import numpy as np
import ml_dtypes

BF16 = ml_dtypes.bfloat16


def bf(x):
    return np.asarray(x, np.float32).astype(BF16)


def f32(x):
    return np.asarray(x, np.float32)


def f64(x):
    return np.asarray(x).astype(np.float64)


def striped(idx):
    return np.tile(idx.reshape(-1, 16).T, (8, 1))


C, S, F, R, K, N = 128, 512, 3, 256, 8, 2048


def setup_inputs():
    return {"spatial_w": f32(np.random.standard_normal((C, S))), "edge_feat": bf(np.random.standard_normal((F, C, N))), "w": bf(np.random.standard_normal((C, C)) * np.sqrt(F / C)), "attn_bias": f32(np.random.standard_normal((1, N))), "offs": striped(np.concatenate([np.random.permutation(S)[:R] for _ in range(K)]))}


def reference(spatial_w, edge_feat, w, attn_bias, offs):
    idx = offs[:16].T.reshape(-1)
    edge = np.einsum("hc,fhn->cn", f64(w), f64(edge_feat)) / F
    return f64(spatial_w)[:, idx] + (edge + 2.0 * f64(attn_bias))

@@ -1,0 +1,55 @@
+import concourse.mybir as mybir
+
+F32 = mybir.dt.float32
+BF16 = mybir.dt.bfloat16
+U16 = mybir.dt.uint16
+ADD = mybir.AluOpType.add
+MULT = mybir.AluOpType.mult
+
+HEADS = 128
+DISTANCES = 512
+FEATURES = 3
+PAIRS = 2048
+CHUNK = 512
+CHUNKS = PAIRS // CHUNK
+OFFSETS_PER_COLUMN = 16
+
+FLOPS = 2 * FEATURES * HEADS * HEADS * PAIRS
+
+
+def tile_graphormergraphattnbias_kernel(tc, spatial_w, edge_feat, w, attn_bias, offs, out):
+    nc = tc.nc
+    with (
+        tc.tile_pool(name="held", bufs=1) as held,
+        tc.psum_pool(name="banks", bufs=1) as banks,
+    ):
+        offsets = held.tile([HEADS, PAIRS // OFFSETS_PER_COLUMN], U16, name="offsets")
+        nc.sync.dma_start(offsets[:], offs)
+        weights = held.tile([HEADS, HEADS], BF16, name="weights")
+        nc.sync.dma_start(weights[:], w)
+        table = held.tile([HEADS, DISTANCES], F32, name="table")
+        nc.scalar.dma_start(table[:], spatial_w)
+
+        for k in range(CHUNKS):
+            pairs = slice(k * CHUNK, (k + 1) * CHUNK)
+
+            features = held.tile([HEADS, FEATURES, CHUNK], BF16, name=f"features{k}")
+            nc.sync.dma_start(features[:], edge_feat[:, :, pairs].rearrange("f h n -> h f n"))
+            bias = held.tile([HEADS, CHUNK], F32, name=f"bias{k}")
+            nc.scalar.dma_start(bias[:], attn_bias[:, pairs].broadcast_to([HEADS, CHUNK]))
+            doubled_bias = held.tile([HEADS, CHUNK], F32, name=f"doubled_bias{k}")
+            nc.scalar.mul(doubled_bias[:], bias[:], 2.0)
+
+            edge_sum = banks.tile([HEADS, CHUNK], F32, name=f"edge_sum{k}")
+            for f in range(FEATURES):
+                nc.tensor.matmul(
+                    edge_sum[:], weights[:], features[:, f, :], start=(f == 0), stop=(f == FEATURES - 1)
+                )
+
+            bracket = held.tile([HEADS, CHUNK], F32, name=f"bracket{k}")
+            nc.vector.scalar_tensor_tensor(bracket[:], edge_sum[:], 1.0 / FEATURES, doubled_bias[:], MULT, ADD)
+
+            chunk_offsets = offsets[:, k * CHUNK // OFFSETS_PER_COLUMN : (k + 1) * CHUNK // OFFSETS_PER_COLUMN]
+            result = held.tile([HEADS, CHUNK], F32, name=f"result{k}")
+            nc.vector.tensor_tensor(result[:], table[:].indirect(chunk_offsets), bracket[:], ADD)
+            nc.sync.dma_start(out[:, pairs], result[:])

@@ -10,11 +10,14 @@ HEADS = 128
 DISTANCES = 512
 FEATURES = 3
 PAIRS = 2048
-CHUNK = 512
-CHUNKS = PAIRS // CHUNK
 OFFSETS_PER_COLUMN = 16
 
 FLOPS = 2 * FEATURES * HEADS * HEADS * PAIRS
+
+CHUNK = 512
+CHUNKS = PAIRS // CHUNK
+PIECE = 256
+PIECES_PER_CHUNK = CHUNK // PIECE
 
 
 def tile_graphormergraphattnbias_kernel(tc, spatial_w, edge_feat, w, attn_bias, offs, out):
@@ -23,33 +26,49 @@ def tile_graphormergraphattnbias_kernel(tc, spatial_w, edge_feat, w, attn_bias, 
         tc.tile_pool(name="held", bufs=1) as held,
         tc.psum_pool(name="banks", bufs=1) as banks,
     ):
-        offsets = held.tile([HEADS, PAIRS // OFFSETS_PER_COLUMN], U16, name="offsets")
-        nc.sync.dma_start(offsets[:], offs)
         weights = held.tile([HEADS, HEADS], BF16, name="weights")
-        nc.sync.dma_start(weights[:], w)
+        nc.scalar.dma_start(weights[:], w)
         table = held.tile([HEADS, DISTANCES], F32, name="table")
         nc.scalar.dma_start(table[:], spatial_w)
-
+        offsets = held.tile([HEADS, PAIRS // OFFSETS_PER_COLUMN], U16, name="offsets")
+        features = []
+        bias = []
         for k in range(CHUNKS):
             pairs = slice(k * CHUNK, (k + 1) * CHUNK)
+            features.append(held.tile([HEADS, FEATURES, CHUNK], BF16, name=f"features{k}"))
+            nc.sync.dma_start(features[k][:], edge_feat[:, :, pairs].rearrange("f h n -> h f n"))
+            bias.append(held.tile([HEADS, CHUNK], F32, name=f"bias{k}"))
+            nc.sync.dma_start(bias[k][:], attn_bias[:, pairs].broadcast_to([HEADS, CHUNK]))
+            if k == 0:
+                nc.sync.dma_start(offsets[:], offs)
 
-            features = held.tile([HEADS, FEATURES, CHUNK], BF16, name=f"features{k}")
-            nc.sync.dma_start(features[:], edge_feat[:, :, pairs].rearrange("f h n -> h f n"))
-            bias = held.tile([HEADS, CHUNK], F32, name=f"bias{k}")
-            nc.scalar.dma_start(bias[:], attn_bias[:, pairs].broadcast_to([HEADS, CHUNK]))
+        constant = held.tile([HEADS, 1], F32, name="constant")
+        nc.vector.memset(constant[:], 0.0)
+        warmed = held.tile([HEADS, 1], F32, name="warmed")
+        nc.scalar.mul(warmed[:], constant[:], 2.0)
+
+        for k in range(CHUNKS):
             doubled_bias = held.tile([HEADS, CHUNK], F32, name=f"doubled_bias{k}")
-            nc.scalar.mul(doubled_bias[:], bias[:], 2.0)
+            nc.scalar.mul(doubled_bias[:], bias[k][:], 2.0)
 
-            edge_sum = banks.tile([HEADS, CHUNK], F32, name=f"edge_sum{k}")
-            for f in range(FEATURES):
-                nc.tensor.matmul(
-                    edge_sum[:], weights[:], features[:, f, :], start=(f == 0), stop=(f == FEATURES - 1)
+            for i in range(PIECES_PER_CHUNK):
+                in_chunk = slice(i * PIECE, (i + 1) * PIECE)
+                first_pair = k * CHUNK + i * PIECE
+
+                edge_sum = banks.tile([HEADS, PIECE], F32, name=f"edge_sum{k}_{i}")
+                for f in range(FEATURES):
+                    nc.tensor.matmul(
+                        edge_sum[:], weights[:], features[k][:, f, in_chunk], start=(f == 0), stop=(f == FEATURES - 1)
+                    )
+
+                bracket = held.tile([HEADS, PIECE], F32, name=f"bracket{k}_{i}")
+                nc.vector.scalar_tensor_tensor(
+                    bracket[:], edge_sum[:], 1.0 / FEATURES, doubled_bias[:, in_chunk], MULT, ADD
                 )
 
-            bracket = held.tile([HEADS, CHUNK], F32, name=f"bracket{k}")
-            nc.vector.scalar_tensor_tensor(bracket[:], edge_sum[:], 1.0 / FEATURES, doubled_bias[:], MULT, ADD)
-
-            chunk_offsets = offsets[:, k * CHUNK // OFFSETS_PER_COLUMN : (k + 1) * CHUNK // OFFSETS_PER_COLUMN]
-            result = held.tile([HEADS, CHUNK], F32, name=f"result{k}")
-            nc.vector.tensor_tensor(result[:], table[:].indirect(chunk_offsets), bracket[:], ADD)
-            nc.sync.dma_start(out[:, pairs], result[:])
+                piece_offsets = offsets[
+                    :, first_pair // OFFSETS_PER_COLUMN : (first_pair + PIECE) // OFFSETS_PER_COLUMN
+                ]
+                result = held.tile([HEADS, PIECE], F32, name=f"result{k}_{i}")
+                nc.vector.tensor_tensor(result[:], table[:].indirect(piece_offsets), bracket[:], ADD)
+                nc.sync.dma_start(out[:, first_pair : first_pair + PIECE], result[:])

@@ -42,14 +42,20 @@ def tile_graphormergraphattnbias_kernel(tc, spatial_w, edge_feat, w, attn_bias, 
             if k == 0:
                 nc.sync.dma_start(offsets[:], offs)
 
+        bias_weights = held.tile([HEADS, HEADS], F32, name="bias_weights")
+        nc.gpsimd.memset(bias_weights[:], 0.0)
+        nc.gpsimd.memset(bias_weights[0:1, :], 2.0 * FEATURES)
+
         constant = held.tile([HEADS, 1], F32, name="constant")
         nc.vector.memset(constant[:], 0.0)
         warmed = held.tile([HEADS, 1], F32, name="warmed")
         nc.scalar.mul(warmed[:], constant[:], 2.0)
 
         for k in range(CHUNKS):
-            doubled_bias = held.tile([HEADS, CHUNK], F32, name=f"doubled_bias{k}")
-            nc.scalar.mul(doubled_bias[:], bias[k][:], 2.0)
+            vector_makes_bracket = k < CHUNKS - 1
+            if vector_makes_bracket:
+                doubled_bias = held.tile([HEADS, CHUNK], F32, name=f"doubled_bias{k}")
+                nc.scalar.mul(doubled_bias[:], bias[k][:], 2.0)
 
             for i in range(PIECES_PER_CHUNK):
                 in_chunk = slice(i * PIECE, (i + 1) * PIECE)
@@ -58,13 +64,21 @@ def tile_graphormergraphattnbias_kernel(tc, spatial_w, edge_feat, w, attn_bias, 
                 edge_sum = banks.tile([HEADS, PIECE], F32, name=f"edge_sum{k}_{i}")
                 for f in range(FEATURES):
                     nc.tensor.matmul(
-                        edge_sum[:], weights[:], features[k][:, f, in_chunk], start=(f == 0), stop=(f == FEATURES - 1)
+                        edge_sum[:],
+                        weights[:],
+                        features[k][:, f, in_chunk],
+                        start=(f == 0),
+                        stop=(f == FEATURES - 1 and vector_makes_bracket),
                     )
 
                 bracket = held.tile([HEADS, PIECE], F32, name=f"bracket{k}_{i}")
-                nc.vector.scalar_tensor_tensor(
-                    bracket[:], edge_sum[:], 1.0 / FEATURES, doubled_bias[:, in_chunk], MULT, ADD
-                )
+                if vector_makes_bracket:
+                    nc.vector.scalar_tensor_tensor(
+                        bracket[:], edge_sum[:], 1.0 / FEATURES, doubled_bias[:, in_chunk], MULT, ADD
+                    )
+                else:
+                    nc.tensor.matmul(edge_sum[:], bias_weights[:], bias[k][:, in_chunk], start=False, stop=True)
+                    nc.scalar.mul(bracket[:], edge_sum[:], 1.0 / FEATURES)
 
                 piece_offsets = offsets[
                     :, first_pair // OFFSETS_PER_COLUMN : (first_pair + PIECE) // OFFSETS_PER_COLUMN

@@ -16,6 +16,7 @@ FLOPS = 2 * FEATURES * HEADS * HEADS * PAIRS
 
 CHUNK = 512
 CHUNKS = PAIRS // CHUNK
+LAST = CHUNKS - 1
 PIECE = 256
 PIECES_PER_CHUNK = CHUNK // PIECE
 
@@ -26,6 +27,11 @@ def tile_graphormergraphattnbias_kernel(tc, spatial_w, edge_feat, w, attn_bias, 
         tc.tile_pool(name="held", bufs=1) as held,
         tc.psum_pool(name="banks", bufs=1) as banks,
     ):
+        last_bias = held.tile([HEADS, CHUNK], F32, name="last_bias")
+        nc.gpsimd.memset(last_bias[:], 0.0)
+        sixes = held.tile([HEADS, HEADS], F32, name="sixes")
+        nc.gpsimd.memset(sixes[:], 2.0 * FEATURES)
+
         weights = held.tile([HEADS, HEADS], BF16, name="weights")
         nc.scalar.dma_start(weights[:], w)
         table = held.tile([HEADS, DISTANCES], F32, name="table")
@@ -37,14 +43,12 @@ def tile_graphormergraphattnbias_kernel(tc, spatial_w, edge_feat, w, attn_bias, 
             pairs = slice(k * CHUNK, (k + 1) * CHUNK)
             features.append(held.tile([HEADS, FEATURES, CHUNK], BF16, name=f"features{k}"))
             nc.sync.dma_start(features[k][:], edge_feat[:, :, pairs].rearrange("f h n -> h f n"))
-            bias.append(held.tile([HEADS, CHUNK], F32, name=f"bias{k}"))
-            nc.sync.dma_start(bias[k][:], attn_bias[:, pairs].broadcast_to([HEADS, CHUNK]))
+            if k < LAST:
+                bias.append(held.tile([HEADS, CHUNK], F32, name=f"bias{k}"))
+                nc.sync.dma_start(bias[k][:], attn_bias[:, pairs].broadcast_to([HEADS, CHUNK]))
             if k == 0:
                 nc.sync.dma_start(offsets[:], offs)
-
-        bias_weights = held.tile([HEADS, HEADS], F32, name="bias_weights")
-        nc.gpsimd.memset(bias_weights[:], 0.0)
-        nc.gpsimd.memset(bias_weights[0:1, :], 2.0 * FEATURES)
+                nc.sync.dma_start(last_bias[0:1, :], attn_bias[:, LAST * CHUNK :])
 
         constant = held.tile([HEADS, 1], F32, name="constant")
         nc.vector.memset(constant[:], 0.0)
@@ -52,8 +56,7 @@ def tile_graphormergraphattnbias_kernel(tc, spatial_w, edge_feat, w, attn_bias, 
         nc.scalar.mul(warmed[:], constant[:], 2.0)
 
         for k in range(CHUNKS):
-            vector_makes_bracket = k < CHUNKS - 1
-            if vector_makes_bracket:
+            if k < LAST:
                 doubled_bias = held.tile([HEADS, CHUNK], F32, name=f"doubled_bias{k}")
                 nc.scalar.mul(doubled_bias[:], bias[k][:], 2.0)
 
@@ -62,22 +65,23 @@ def tile_graphormergraphattnbias_kernel(tc, spatial_w, edge_feat, w, attn_bias, 
                 first_pair = k * CHUNK + i * PIECE
 
                 edge_sum = banks.tile([HEADS, PIECE], F32, name=f"edge_sum{k}_{i}")
+                if k == LAST:
+                    nc.tensor.matmul(edge_sum[:], sixes[:], last_bias[:, in_chunk], start=True, stop=False)
                 for f in range(FEATURES):
                     nc.tensor.matmul(
                         edge_sum[:],
                         weights[:],
                         features[k][:, f, in_chunk],
-                        start=(f == 0),
-                        stop=(f == FEATURES - 1 and vector_makes_bracket),
+                        start=(f == 0 and k < LAST),
+                        stop=(f == FEATURES - 1),
                     )
 
                 bracket = held.tile([HEADS, PIECE], F32, name=f"bracket{k}_{i}")
-                if vector_makes_bracket:
+                if k < LAST:
                     nc.vector.scalar_tensor_tensor(
                         bracket[:], edge_sum[:], 1.0 / FEATURES, doubled_bias[:, in_chunk], MULT, ADD
                     )
                 else:
-                    nc.tensor.matmul(edge_sum[:], bias_weights[:], bias[k][:, in_chunk], start=False, stop=True)
                     nc.scalar.mul(bracket[:], edge_sum[:], 1.0 / FEATURES)
 
                 piece_offsets = offsets[

@@ -16,7 +16,8 @@ FLOPS = 2 * FEATURES * HEADS * HEADS * PAIRS
 
 CHUNK = 512
 CHUNKS = PAIRS // CHUNK
-LAST = CHUNKS - 1
+VECTOR_CHUNKS = 2
+VECTOR_PAIRS = VECTOR_CHUNKS * CHUNK
 PIECE = 256
 PIECES_PER_CHUNK = CHUNK // PIECE
 
@@ -25,10 +26,10 @@ def tile_graphormergraphattnbias_kernel(tc, spatial_w, edge_feat, w, attn_bias, 
     nc = tc.nc
     with (
         tc.tile_pool(name="held", bufs=1) as held,
-        tc.psum_pool(name="banks", bufs=1) as banks,
+        tc.psum_pool(name="banks", bufs=8) as banks,
     ):
-        last_bias = held.tile([HEADS, CHUNK], F32, name="last_bias")
-        nc.gpsimd.memset(last_bias[:], 0.0)
+        bias_row = held.tile([HEADS, PAIRS - VECTOR_PAIRS], F32, name="bias_row")
+        nc.gpsimd.memset(bias_row[:], 0.0)
         sixes = held.tile([HEADS, HEADS], F32, name="sixes")
         nc.gpsimd.memset(sixes[:], 2.0 * FEATURES)
 
@@ -43,12 +44,12 @@ def tile_graphormergraphattnbias_kernel(tc, spatial_w, edge_feat, w, attn_bias, 
             pairs = slice(k * CHUNK, (k + 1) * CHUNK)
             features.append(held.tile([HEADS, FEATURES, CHUNK], BF16, name=f"features{k}"))
             nc.sync.dma_start(features[k][:], edge_feat[:, :, pairs].rearrange("f h n -> h f n"))
-            if k < LAST:
+            if k < VECTOR_CHUNKS:
                 bias.append(held.tile([HEADS, CHUNK], F32, name=f"bias{k}"))
                 nc.sync.dma_start(bias[k][:], attn_bias[:, pairs].broadcast_to([HEADS, CHUNK]))
             if k == 0:
                 nc.sync.dma_start(offsets[:], offs)
-                nc.sync.dma_start(last_bias[0:1, :], attn_bias[:, LAST * CHUNK :])
+                nc.sync.dma_start(bias_row[0:1, :], attn_bias[:, VECTOR_PAIRS:])
 
         constant = held.tile([HEADS, 1], F32, name="constant")
         nc.vector.memset(constant[:], 0.0)
@@ -56,7 +57,8 @@ def tile_graphormergraphattnbias_kernel(tc, spatial_w, edge_feat, w, attn_bias, 
         nc.scalar.mul(warmed[:], constant[:], 2.0)
 
         for k in range(CHUNKS):
-            if k < LAST:
+            vector_makes_brackets = k < VECTOR_CHUNKS
+            if vector_makes_brackets:
                 doubled_bias = held.tile([HEADS, CHUNK], F32, name=f"doubled_bias{k}")
                 nc.scalar.mul(doubled_bias[:], bias[k][:], 2.0)
 
@@ -64,20 +66,21 @@ def tile_graphormergraphattnbias_kernel(tc, spatial_w, edge_feat, w, attn_bias, 
                 in_chunk = slice(i * PIECE, (i + 1) * PIECE)
                 first_pair = k * CHUNK + i * PIECE
 
-                edge_sum = banks.tile([HEADS, PIECE], F32, name=f"edge_sum{k}_{i}")
-                if k == LAST:
-                    nc.tensor.matmul(edge_sum[:], sixes[:], last_bias[:, in_chunk], start=True, stop=False)
+                edge_sum = banks.tile([HEADS, PIECE], F32, name="edge_sum")
+                if not vector_makes_brackets:
+                    in_row = slice(first_pair - VECTOR_PAIRS, first_pair - VECTOR_PAIRS + PIECE)
+                    nc.tensor.matmul(edge_sum[:], sixes[:], bias_row[:, in_row], start=True, stop=False)
                 for f in range(FEATURES):
                     nc.tensor.matmul(
                         edge_sum[:],
                         weights[:],
                         features[k][:, f, in_chunk],
-                        start=(f == 0 and k < LAST),
+                        start=(f == 0 and vector_makes_brackets),
                         stop=(f == FEATURES - 1),
                     )
 
                 bracket = held.tile([HEADS, PIECE], F32, name=f"bracket{k}_{i}")
-                if k < LAST:
+                if vector_makes_brackets:
                     nc.vector.scalar_tensor_tensor(
                         bracket[:], edge_sum[:], 1.0 / FEATURES, doubled_bias[:, in_chunk], MULT, ADD
                     )

@@ -20,13 +20,16 @@ VECTOR_CHUNKS = 2
 VECTOR_PAIRS = VECTOR_CHUNKS * CHUNK
 PIECE = 256
 PIECES_PER_CHUNK = CHUNK // PIECE
+WARM_UP_COLUMNS = 512
+WARM_UP_MATMULS = 4
 
 
 def tile_graphormergraphattnbias_kernel(tc, spatial_w, edge_feat, w, attn_bias, offs, out):
     nc = tc.nc
     with (
         tc.tile_pool(name="held", bufs=1) as held,
-        tc.psum_pool(name="banks", bufs=8) as banks,
+        tc.psum_pool(name="banks", bufs=7) as banks,
+        tc.psum_pool(name="spare", bufs=1) as spare,
     ):
         bias_row = held.tile([HEADS, PAIRS - VECTOR_PAIRS], F32, name="bias_row")
         nc.gpsimd.memset(bias_row[:], 0.0)
@@ -55,6 +58,12 @@ def tile_graphormergraphattnbias_kernel(tc, spatial_w, edge_feat, w, attn_bias, 
         nc.vector.memset(constant[:], 0.0)
         warmed = held.tile([HEADS, 1], F32, name="warmed")
         nc.scalar.mul(warmed[:], constant[:], 2.0)
+
+        zeros = held.tile([HEADS, WARM_UP_COLUMNS], BF16, name="zeros")
+        nc.vector.memset(zeros[:], 0.0)
+        unused = spare.tile([HEADS, WARM_UP_COLUMNS], F32, name="unused")
+        for repeat in range(WARM_UP_MATMULS):
+            nc.tensor.matmul(unused[:], zeros[:, 0:HEADS], zeros[:], start=True, stop=True)
 
         for k in range(CHUNKS):
             vector_makes_brackets = k < VECTOR_CHUNKS

@@ -1,10 +1,10 @@
 import concourse.mybir as mybir
+from concourse.masks import make_identity
 
 F32 = mybir.dt.float32
 BF16 = mybir.dt.bfloat16
 U16 = mybir.dt.uint16
 ADD = mybir.AluOpType.add
-MULT = mybir.AluOpType.mult
 
 HEADS = 128
 DISTANCES = 512
@@ -16,12 +16,12 @@ FLOPS = 2 * FEATURES * HEADS * HEADS * PAIRS
 
 CHUNK = 512
 CHUNKS = PAIRS // CHUNK
-VECTOR_CHUNKS = 2
-VECTOR_PAIRS = VECTOR_CHUNKS * CHUNK
 PIECE = 256
 PIECES_PER_CHUNK = CHUNK // PIECE
-WARM_UP_COLUMNS = 512
-WARM_UP_MATMULS = 4
+BLOCK = 128
+BLOCKS = PAIRS // BLOCK
+BLOCKS_PER_PIECE = PIECE // BLOCK
+ROWS = 64
 
 
 def tile_graphormergraphattnbias_kernel(tc, spatial_w, edge_feat, w, attn_bias, offs, out):
@@ -29,72 +29,60 @@ def tile_graphormergraphattnbias_kernel(tc, spatial_w, edge_feat, w, attn_bias, 
     with (
         tc.tile_pool(name="held", bufs=1) as held,
         tc.psum_pool(name="banks", bufs=7) as banks,
-        tc.psum_pool(name="spare", bufs=1) as spare,
+        tc.psum_pool(name="flip", bufs=1) as flip,
     ):
-        bias_row = held.tile([HEADS, PAIRS - VECTOR_PAIRS], F32, name="bias_row")
-        nc.gpsimd.memset(bias_row[:], 0.0)
-        sixes = held.tile([HEADS, HEADS], F32, name="sixes")
-        nc.gpsimd.memset(sixes[:], 2.0 * FEATURES)
+        bias_rows = held.tile([ROWS, BLOCK], F32, name="bias_rows")
+        nc.gpsimd.memset(bias_rows[:], 0.0)
+        identity = held.tile([HEADS, HEADS], F32, name="identity")
+        make_identity(nc, identity[:])
 
+        nc.sync.dma_start(bias_rows[0:BLOCKS, :], attn_bias.rearrange("o (a p) -> (o a) p", p=BLOCK))
         weights = held.tile([HEADS, HEADS], BF16, name="weights")
-        nc.scalar.dma_start(weights[:], w)
-        table = held.tile([HEADS, DISTANCES], F32, name="table")
-        nc.scalar.dma_start(table[:], spatial_w)
+        nc.sync.dma_start(weights[:], w)
         offsets = held.tile([HEADS, PAIRS // OFFSETS_PER_COLUMN], U16, name="offsets")
+        table = held.tile([HEADS, DISTANCES], F32, name="table")
         features = []
-        bias = []
         for k in range(CHUNKS):
             pairs = slice(k * CHUNK, (k + 1) * CHUNK)
             features.append(held.tile([HEADS, FEATURES, CHUNK], BF16, name=f"features{k}"))
             nc.sync.dma_start(features[k][:], edge_feat[:, :, pairs].rearrange("f h n -> h f n"))
-            if k < VECTOR_CHUNKS:
-                bias.append(held.tile([HEADS, CHUNK], F32, name=f"bias{k}"))
-                nc.sync.dma_start(bias[k][:], attn_bias[:, pairs].broadcast_to([HEADS, CHUNK]))
             if k == 0:
                 nc.sync.dma_start(offsets[:], offs)
-                nc.sync.dma_start(bias_row[0:1, :], attn_bias[:, VECTOR_PAIRS:])
+                nc.sync.dma_start(table[:], spatial_w)
 
         constant = held.tile([HEADS, 1], F32, name="constant")
         nc.vector.memset(constant[:], 0.0)
         warmed = held.tile([HEADS, 1], F32, name="warmed")
         nc.scalar.mul(warmed[:], constant[:], 2.0)
 
-        zeros = held.tile([HEADS, WARM_UP_COLUMNS], BF16, name="zeros")
-        nc.vector.memset(zeros[:], 0.0)
-        unused = spare.tile([HEADS, WARM_UP_COLUMNS], F32, name="unused")
-        for repeat in range(WARM_UP_MATMULS):
-            nc.tensor.matmul(unused[:], zeros[:, 0:HEADS], zeros[:], start=True, stop=True)
+        bias_columns = flip.tile([BLOCK, ROWS], F32, name="bias_columns")
+        nc.tensor.transpose(bias_columns[:], bias_rows[:], identity[0:ROWS, 0:ROWS])
+        six_bias = held.tile([BLOCK, BLOCKS], F32, name="six_bias")
+        nc.vector.tensor_scalar_mul(six_bias[:], bias_columns[:, 0:BLOCKS], 2.0 * FEATURES)
 
         for k in range(CHUNKS):
-            vector_makes_brackets = k < VECTOR_CHUNKS
-            if vector_makes_brackets:
-                doubled_bias = held.tile([HEADS, CHUNK], F32, name=f"doubled_bias{k}")
-                nc.scalar.mul(doubled_bias[:], bias[k][:], 2.0)
-
             for i in range(PIECES_PER_CHUNK):
                 in_chunk = slice(i * PIECE, (i + 1) * PIECE)
                 first_pair = k * CHUNK + i * PIECE
 
                 edge_sum = banks.tile([HEADS, PIECE], F32, name="edge_sum")
-                if not vector_makes_brackets:
-                    in_row = slice(first_pair - VECTOR_PAIRS, first_pair - VECTOR_PAIRS + PIECE)
-                    nc.tensor.matmul(edge_sum[:], sixes[:], bias_row[:, in_row], start=True, stop=False)
+                for b in range(BLOCKS_PER_PIECE):
+                    block = first_pair // BLOCK + b
+                    nc.tensor.matmul(
+                        edge_sum[:, b * BLOCK : (b + 1) * BLOCK],
+                        six_bias[:, block : block + 1].to_broadcast([BLOCK, HEADS]),
+                        identity[:],
+                        is_transpose=True,
+                        start=(b == 0),
+                        stop=False,
+                    )
                 for f in range(FEATURES):
                     nc.tensor.matmul(
-                        edge_sum[:],
-                        weights[:],
-                        features[k][:, f, in_chunk],
-                        start=(f == 0 and vector_makes_brackets),
-                        stop=(f == FEATURES - 1),
+                        edge_sum[:], weights[:], features[k][:, f, in_chunk], start=False, stop=(f == FEATURES - 1)
                     )
 
                 bracket = held.tile([HEADS, PIECE], F32, name=f"bracket{k}_{i}")
-                if vector_makes_brackets:
-                    nc.vector.scalar_tensor_tensor(
-                        bracket[:], edge_sum[:], 1.0 / FEATURES, doubled_bias[:, in_chunk], MULT, ADD
-                    )
-                else:
-                    nc.scalar.mul(bracket[:], edge_sum[:], 1.0 / FEATURES)
+                nc.scalar.mul(bracket[:], edge_sum[:], 1.0 / FEATURES)
 
                 piece_offsets = offsets[
                     :, first_pair // OFFSETS_PER_COLUMN : (first_pair + PIECE) // OFFSETS_PER_COLUMN

@@ -61,6 +61,7 @@ def tile_graphormergraphattnbias_kernel(tc, spatial_w, edge_feat, w, attn_bias, 
         nc.vector.tensor_scalar_mul(six_bias[:], bias_columns[:, 0:BLOCKS], 2.0 * FEATURES)
 
         for k in range(CHUNKS):
+            result = held.tile([HEADS, CHUNK], F32, name=f"result{k}")
             for i in range(PIECES_PER_CHUNK):
                 in_chunk = slice(i * PIECE, (i + 1) * PIECE)
                 first_pair = k * CHUNK + i * PIECE
@@ -87,6 +88,9 @@ def tile_graphormergraphattnbias_kernel(tc, spatial_w, edge_feat, w, attn_bias, 
                 piece_offsets = offsets[
                     :, first_pair // OFFSETS_PER_COLUMN : (first_pair + PIECE) // OFFSETS_PER_COLUMN
                 ]
-                result = held.tile([HEADS, PIECE], F32, name=f"result{k}_{i}")
-                nc.vector.tensor_tensor(result[:], table[:].indirect(piece_offsets), bracket[:], ADD)
-                nc.sync.dma_start(out[:, first_pair : first_pair + PIECE], result[:])
+                nc.vector.tensor_tensor(result[:, in_chunk], table[:].indirect(piece_offsets), bracket[:], ADD)
+
+                if k == CHUNKS - 1:
+                    nc.sync.dma_start(out[:, first_pair : first_pair + PIECE], result[:, in_chunk])
+                elif i == PIECES_PER_CHUNK - 1:
+                    nc.sync.dma_start(out[:, k * CHUNK : (k + 1) * CHUNK], result[:])

@@ -14,10 +14,11 @@ OFFSETS_PER_COLUMN = 16
 
 FLOPS = 2 * FEATURES * HEADS * HEADS * PAIRS
 
-CHUNK = 512
-CHUNKS = PAIRS // CHUNK
 PIECE = 256
-PIECES_PER_CHUNK = CHUNK // PIECE
+PIECES = PAIRS // PIECE
+LOADS = (512, 512, 512, 512)
+STORE = 512
+PIECES_PER_STORE = STORE // PIECE
 BLOCK = 128
 BLOCKS = PAIRS // BLOCK
 BLOCKS_PER_PIECE = PIECE // BLOCK
@@ -41,56 +42,64 @@ def tile_graphormergraphattnbias_kernel(tc, spatial_w, edge_feat, w, attn_bias, 
         nc.sync.dma_start(weights[:], w)
         offsets = held.tile([HEADS, PAIRS // OFFSETS_PER_COLUMN], U16, name="offsets")
         table = held.tile([HEADS, DISTANCES], F32, name="table")
-        features = []
-        for k in range(CHUNKS):
-            pairs = slice(k * CHUNK, (k + 1) * CHUNK)
-            features.append(held.tile([HEADS, FEATURES, CHUNK], BF16, name=f"features{k}"))
-            nc.sync.dma_start(features[k][:], edge_feat[:, :, pairs].rearrange("f h n -> h f n"))
+        features_of_piece = []
+        first_pair = 0
+        for k, pairs in enumerate(LOADS):
+            features = held.tile([HEADS, FEATURES, pairs], BF16, name=f"features{k}")
+            nc.sync.dma_start(
+                features[:], edge_feat[:, :, first_pair : first_pair + pairs].rearrange("f h n -> h f n")
+            )
+            for i in range(pairs // PIECE):
+                features_of_piece.append([features[:, f, i * PIECE : (i + 1) * PIECE] for f in range(FEATURES)])
+            first_pair += pairs
             if k == 0:
                 nc.sync.dma_start(offsets[:], offs)
                 nc.sync.dma_start(table[:], spatial_w)
-
-        constant = held.tile([HEADS, 1], F32, name="constant")
-        nc.vector.memset(constant[:], 0.0)
-        warmed = held.tile([HEADS, 1], F32, name="warmed")
-        nc.scalar.mul(warmed[:], constant[:], 2.0)
 
         bias_columns = flip.tile([BLOCK, ROWS], F32, name="bias_columns")
         nc.tensor.transpose(bias_columns[:], bias_rows[:], identity[0:ROWS, 0:ROWS])
         six_bias = held.tile([BLOCK, BLOCKS], F32, name="six_bias")
         nc.vector.tensor_scalar_mul(six_bias[:], bias_columns[:, 0:BLOCKS], 2.0 * FEATURES)
 
-        for k in range(CHUNKS):
-            result = held.tile([HEADS, CHUNK], F32, name=f"result{k}")
-            for i in range(PIECES_PER_CHUNK):
-                in_chunk = slice(i * PIECE, (i + 1) * PIECE)
-                first_pair = k * CHUNK + i * PIECE
+        def add_bias(edge_sum, piece, opens):
+            for b in range(BLOCKS_PER_PIECE):
+                block = piece * BLOCKS_PER_PIECE + b
+                nc.tensor.matmul(
+                    edge_sum[:, b * BLOCK : (b + 1) * BLOCK],
+                    six_bias[:, block : block + 1].to_broadcast([BLOCK, HEADS]),
+                    identity[:],
+                    is_transpose=True,
+                    start=(opens and b == 0),
+                    stop=(not opens and b == BLOCKS_PER_PIECE - 1),
+                )
 
-                edge_sum = banks.tile([HEADS, PIECE], F32, name="edge_sum")
-                for b in range(BLOCKS_PER_PIECE):
-                    block = first_pair // BLOCK + b
-                    nc.tensor.matmul(
-                        edge_sum[:, b * BLOCK : (b + 1) * BLOCK],
-                        six_bias[:, block : block + 1].to_broadcast([BLOCK, HEADS]),
-                        identity[:],
-                        is_transpose=True,
-                        start=(b == 0),
-                        stop=False,
-                    )
-                for f in range(FEATURES):
-                    nc.tensor.matmul(
-                        edge_sum[:], weights[:], features[k][:, f, in_chunk], start=False, stop=(f == FEATURES - 1)
-                    )
+        def add_features(edge_sum, piece, opens):
+            for f in range(FEATURES):
+                nc.tensor.matmul(
+                    edge_sum[:],
+                    weights[:],
+                    features_of_piece[piece][f],
+                    start=(opens and f == 0),
+                    stop=(not opens and f == FEATURES - 1),
+                )
 
-                bracket = held.tile([HEADS, PIECE], F32, name=f"bracket{k}_{i}")
-                nc.scalar.mul(bracket[:], edge_sum[:], 1.0 / FEATURES)
+        for piece in range(PIECES):
+            first_pair = piece * PIECE
+            if piece % PIECES_PER_STORE == 0:
+                result = held.tile([HEADS, STORE], F32, name=f"result{piece // PIECES_PER_STORE}")
+            in_store = slice((piece % PIECES_PER_STORE) * PIECE, (piece % PIECES_PER_STORE + 1) * PIECE)
 
-                piece_offsets = offsets[
-                    :, first_pair // OFFSETS_PER_COLUMN : (first_pair + PIECE) // OFFSETS_PER_COLUMN
-                ]
-                nc.vector.tensor_tensor(result[:, in_chunk], table[:].indirect(piece_offsets), bracket[:], ADD)
+            edge_sum = banks.tile([HEADS, PIECE], F32, name="edge_sum")
+            add_bias(edge_sum, piece, True)
+            add_features(edge_sum, piece, False)
 
-                if k == CHUNKS - 1:
-                    nc.sync.dma_start(out[:, first_pair : first_pair + PIECE], result[:, in_chunk])
-                elif i == PIECES_PER_CHUNK - 1:
-                    nc.sync.dma_start(out[:, k * CHUNK : (k + 1) * CHUNK], result[:])
+            bracket = held.tile([HEADS, PIECE], F32, name=f"bracket{piece}")
+            nc.scalar.mul(bracket[:], edge_sum[:], 1.0 / FEATURES)
+
+            piece_offsets = offsets[:, first_pair // OFFSETS_PER_COLUMN : (first_pair + PIECE) // OFFSETS_PER_COLUMN]
+            nc.vector.tensor_tensor(result[:, in_store], table[:].indirect(piece_offsets), bracket[:], ADD)
+
+            if piece >= PIECES - PIECES_PER_STORE:
+                nc.sync.dma_start(out[:, first_pair : first_pair + PIECE], result[:, in_store])
+            elif piece % PIECES_PER_STORE == PIECES_PER_STORE - 1:
+                nc.sync.dma_start(out[:, first_pair + PIECE - STORE : first_pair + PIECE], result[:])

@@ -23,6 +23,7 @@ BLOCK = 128
 BLOCKS = PAIRS // BLOCK
 BLOCKS_PER_PIECE = PIECE // BLOCK
 ROWS = 64
+DIRECT = BLOCKS_PER_PIECE
 
 
 def tile_graphormergraphattnbias_kernel(tc, spatial_w, edge_feat, w, attn_bias, offs, out):
@@ -32,7 +33,7 @@ def tile_graphormergraphattnbias_kernel(tc, spatial_w, edge_feat, w, attn_bias, 
         tc.psum_pool(name="banks", bufs=7) as banks,
         tc.psum_pool(name="flip", bufs=1) as flip,
     ):
-        bias_rows = held.tile([ROWS, BLOCK], F32, name="bias_rows")
+        bias_rows = held.tile([HEADS, BLOCK], F32, name="bias_rows")
         nc.gpsimd.memset(bias_rows[:], 0.0)
         identity = held.tile([HEADS, HEADS], F32, name="identity")
         make_identity(nc, identity[:])
@@ -56,22 +57,31 @@ def tile_graphormergraphattnbias_kernel(tc, spatial_w, edge_feat, w, attn_bias, 
                 nc.sync.dma_start(offsets[:], offs)
                 nc.sync.dma_start(table[:], spatial_w)
 
+        six_selector = held.tile([HEADS, 1], F32, name="six_selector")
+        nc.vector.tensor_scalar_mul(six_selector[:], identity[:, DIRECT : DIRECT + 1], 2.0 * FEATURES)
+
         bias_columns = flip.tile([BLOCK, ROWS], F32, name="bias_columns")
-        nc.tensor.transpose(bias_columns[:], bias_rows[:], identity[0:ROWS, 0:ROWS])
+        nc.tensor.transpose(bias_columns[:], bias_rows[0:ROWS, :], identity[0:ROWS, 0:ROWS])
         six_bias = held.tile([BLOCK, BLOCKS], F32, name="six_bias")
         nc.vector.tensor_scalar_mul(six_bias[:], bias_columns[:, 0:BLOCKS], 2.0 * FEATURES)
+
+        direct_sum = banks.tile([HEADS, PIECE], F32, name="edge_sum")
+        nc.tensor.matmul(
+            direct_sum[:, 0:BLOCK], six_selector[:].to_broadcast([HEADS, HEADS]), bias_rows[:], start=True, stop=False
+        )
 
         def add_bias(edge_sum, piece, opens):
             for b in range(BLOCKS_PER_PIECE):
                 block = piece * BLOCKS_PER_PIECE + b
-                nc.tensor.matmul(
-                    edge_sum[:, b * BLOCK : (b + 1) * BLOCK],
-                    six_bias[:, block : block + 1].to_broadcast([BLOCK, HEADS]),
-                    identity[:],
-                    is_transpose=True,
-                    start=(opens and b == 0),
-                    stop=(not opens and b == BLOCKS_PER_PIECE - 1),
-                )
+                if block != DIRECT:
+                    nc.tensor.matmul(
+                        edge_sum[:, b * BLOCK : (b + 1) * BLOCK],
+                        six_bias[:, block : block + 1].to_broadcast([BLOCK, HEADS]),
+                        identity[:],
+                        is_transpose=True,
+                        start=(b == 0),
+                        stop=False,
+                    )
 
         def add_features(edge_sum, piece, opens):
             for f in range(FEATURES):
@@ -89,7 +99,7 @@ def tile_graphormergraphattnbias_kernel(tc, spatial_w, edge_feat, w, attn_bias, 
                 result = held.tile([HEADS, STORE], F32, name=f"result{piece // PIECES_PER_STORE}")
             in_store = slice((piece % PIECES_PER_STORE) * PIECE, (piece % PIECES_PER_STORE + 1) * PIECE)
 
-            edge_sum = banks.tile([HEADS, PIECE], F32, name="edge_sum")
+            edge_sum = direct_sum if piece == DIRECT // BLOCKS_PER_PIECE else banks.tile([HEADS, PIECE], F32, name="edge_sum")
             add_bias(edge_sum, piece, True)
             add_features(edge_sum, piece, False)
 

import concourse.mybir as mybir
from concourse.masks import make_identity

F32 = mybir.dt.float32
BF16 = mybir.dt.bfloat16
U16 = mybir.dt.uint16
ADD = mybir.AluOpType.add

HEADS = 128
DISTANCES = 512
FEATURES = 3
PAIRS = 2048
OFFSETS_PER_COLUMN = 16

FLOPS = 2 * FEATURES * HEADS * HEADS * PAIRS

PIECE = 256
PIECES = PAIRS // PIECE
LOADS = (512, 512, 512, 512)
STORE = 512
PIECES_PER_STORE = STORE // PIECE
BLOCK = 128
BLOCKS = PAIRS // BLOCK
BLOCKS_PER_PIECE = PIECE // BLOCK
ROWS = 64
DIRECT = BLOCKS_PER_PIECE


def tile_graphormergraphattnbias_kernel(tc, spatial_w, edge_feat, w, attn_bias, offs, out):
    nc = tc.nc
    with (
        tc.tile_pool(name="held", bufs=1) as held,
        tc.psum_pool(name="banks", bufs=7) as banks,
        tc.psum_pool(name="flip", bufs=1) as flip,
    ):
        bias_rows = held.tile([HEADS, BLOCK], F32, name="bias_rows")
        nc.gpsimd.memset(bias_rows[:], 0.0)
        identity = held.tile([HEADS, HEADS], F32, name="identity")
        make_identity(nc, identity[:])

        nc.sync.dma_start(bias_rows[0:BLOCKS, :], attn_bias.rearrange("o (a p) -> (o a) p", p=BLOCK))
        weights = held.tile([HEADS, HEADS], BF16, name="weights")
        nc.sync.dma_start(weights[:], w)
        offsets = held.tile([HEADS, PAIRS // OFFSETS_PER_COLUMN], U16, name="offsets")
        table = held.tile([HEADS, DISTANCES], F32, name="table")
        features_of_piece = []
        first_pair = 0
        for k, pairs in enumerate(LOADS):
            features = held.tile([HEADS, FEATURES, pairs], BF16, name=f"features{k}")
            nc.sync.dma_start(
                features[:], edge_feat[:, :, first_pair : first_pair + pairs].rearrange("f h n -> h f n")
            )
            for i in range(pairs // PIECE):
                features_of_piece.append([features[:, f, i * PIECE : (i + 1) * PIECE] for f in range(FEATURES)])
            first_pair += pairs
            if k == 0:
                nc.sync.dma_start(offsets[:], offs)
                nc.sync.dma_start(table[:], spatial_w)

        six_selector = held.tile([HEADS, 1], F32, name="six_selector")
        nc.vector.tensor_scalar_mul(six_selector[:], identity[:, DIRECT : DIRECT + 1], 2.0 * FEATURES)

        bias_columns = flip.tile([BLOCK, ROWS], F32, name="bias_columns")
        nc.tensor.transpose(bias_columns[:], bias_rows[0:ROWS, :], identity[0:ROWS, 0:ROWS])
        six_bias = held.tile([BLOCK, BLOCKS], F32, name="six_bias")
        nc.vector.tensor_scalar_mul(six_bias[:], bias_columns[:, 0:BLOCKS], 2.0 * FEATURES)

        direct_sum = banks.tile([HEADS, PIECE], F32, name="edge_sum")
        nc.tensor.matmul(
            direct_sum[:, 0:BLOCK], six_selector[:].to_broadcast([HEADS, HEADS]), bias_rows[:], start=True, stop=False
        )

        def add_bias(edge_sum, piece, opens):
            for b in range(BLOCKS_PER_PIECE):
                block = piece * BLOCKS_PER_PIECE + b
                if block != DIRECT:
                    nc.tensor.matmul(
                        edge_sum[:, b * BLOCK : (b + 1) * BLOCK],
                        six_bias[:, block : block + 1].to_broadcast([BLOCK, HEADS]),
                        identity[:],
                        is_transpose=True,
                        start=(b == 0),
                        stop=False,
                    )

        def add_features(edge_sum, piece, opens):
            for f in range(FEATURES):
                nc.tensor.matmul(
                    edge_sum[:],
                    weights[:],
                    features_of_piece[piece][f],
                    start=(opens and f == 0),
                    stop=(not opens and f == FEATURES - 1),
                )

        for piece in range(PIECES):
            first_pair = piece * PIECE
            if piece % PIECES_PER_STORE == 0:
                result = held.tile([HEADS, STORE], F32, name=f"result{piece // PIECES_PER_STORE}")
            in_store = slice((piece % PIECES_PER_STORE) * PIECE, (piece % PIECES_PER_STORE + 1) * PIECE)

            edge_sum = direct_sum if piece == DIRECT // BLOCKS_PER_PIECE else banks.tile([HEADS, PIECE], F32, name="edge_sum")
            add_bias(edge_sum, piece, True)
            add_features(edge_sum, piece, False)

            bracket = held.tile([HEADS, PIECE], F32, name=f"bracket{piece}")
            nc.scalar.mul(bracket[:], edge_sum[:], 1.0 / FEATURES)

            piece_offsets = offsets[:, first_pair // OFFSETS_PER_COLUMN : (first_pair + PIECE) // OFFSETS_PER_COLUMN]
            nc.vector.tensor_tensor(result[:, in_store], table[:].indirect(piece_offsets), bracket[:], ADD)

            if piece >= PIECES - PIECES_PER_STORE:
                nc.sync.dma_start(out[:, first_pair : first_pair + PIECE], result[:, in_store])
            elif piece % PIECES_PER_STORE == PIECES_PER_STORE - 1:
                nc.sync.dma_start(out[:, first_pair + PIECE - STORE : first_pair + PIECE], result[:])
